import numpy as np
import ml_dtypes


def mxq(x, axis, fmt="e4m3"):
    dtype, down = {"e4m3": (ml_dtypes.float8_e4m3fn, 7), "e5m2": (ml_dtypes.float8_e5m2, 14)}[fmt]
    v = np.moveaxis(np.asarray(x, np.float32).astype(ml_dtypes.bfloat16).astype(np.float64), axis, -1)
    blocks = v.reshape(v.shape[:-1] + (-1, 32))
    amax = np.abs(blocks).max(-1, keepdims=True)
    byte = np.maximum(np.where(amax > 0, np.frexp(amax)[1] - 1 + 127, 0) - down, 1)
    scale = np.exp2(byte - 127.0)
    codes = (blocks / scale).astype(np.float32).astype(dtype).astype(np.float64)
    return np.moveaxis((codes * scale).reshape(v.shape), -1, axis)


WIDE = False


def mx_kscale(k):
    if not WIDE:
        return np.ones(k)
    levels = np.array([20, -20, 10, -10, 0])
    a = np.random.permutation(np.resize(levels, k // 512 * 4)).reshape(k // 512, 4)
    idx = np.arange(k)
    return np.exp2(a[idx // 512, idx % 128 // 32])


BF16 = ml_dtypes.bfloat16


def bf(x):
    return np.asarray(x, np.float32).astype(BF16)


def f64(x):
    return np.asarray(x).astype(np.float64)


B, IN_C, OUT_C, H, W, K, STRIDE, PAD = 512, 128, 512, 3, 3, 3, 1, 1
OH = (H + 2 * PAD - K) // STRIDE + 1
OW = (W + 2 * PAD - K) // STRIDE + 1


def _span(t, n_in, n_out):
    lo = max(0, -((t - PAD) // STRIDE))
    hi = min(n_out, (n_in - 1 + PAD - t) // STRIDE + 1)
    return lo, hi


def setup_inputs():
    s = mx_kscale(B)[:, None, None, None]
    x = np.random.standard_normal((B, IN_C, H, W)) * s
    weights = np.random.uniform(0.0, 1.0, (OH, OW, OUT_C, IN_C, K, K)) * (1.7 / np.sqrt(IN_C * K * K))
    bias = np.random.uniform(0.0, 1.0, (OUT_C, OH, OW))
    g = np.random.standard_normal((B, OUT_C, OH, OW)) * np.exp2(np.random.randint(-12, 1, (B, 1, OH, OW))) / s
    return {"x": bf(x), "weights": bf(weights), "bias": bf(bias), "grad_out": bf(g)}


def reference(x, weights, bias, grad_out):
    xq = mxq(f64(x), 0, "e4m3")
    gq = mxq(f64(grad_out), 0, "e5m2")
    out = np.zeros((OH, OW, OUT_C, IN_C, K, K))
    for i in range(K):
        h0, h1 = _span(i, H, OH)
        for j in range(K):
            w0, w1 = _span(j, W, OW)
            xs = xq[:, :, h0 * STRIDE + i - PAD:(h1 - 1) * STRIDE + i - PAD + 1:STRIDE,
                    w0 * STRIDE + j - PAD:(w1 - 1) * STRIDE + j - PAD + 1:STRIDE]
            gs = gq[:, :, h0:h1, w0:w1]
            out[h0:h1, w0:w1, :, :, i, j] = gs.transpose(2, 3, 1, 0) @ xs.transpose(2, 3, 0, 1)
    return out

@@ -1,0 +1,144 @@
+from contextlib import ExitStack
+
+import concourse.mybir as mybir
+
+BF16 = mybir.dt.bfloat16
+F32 = mybir.dt.float32
+I32 = mybir.dt.int32
+U8 = mybir.dt.uint8
+E4X4 = mybir.dt.float8_e4m3fn_x4
+E5X4 = mybir.dt.float8_e5m2_x4
+
+P = 128
+PACK = 4
+B, IN_C, OUT_C, SIDE = 512, 128, 512, 3
+LOCS = SIDE * SIDE
+XCOLS = IN_C * LOCS
+O_TILES = OUT_C // P
+PAD = 64
+WIN = 512
+STEP = 384
+XWIDE = 2 * STEP + WIN
+GROUP = 3
+
+FLOPS = 2 * 49 * OUT_C * IN_C * B
+BYTES = 2 * B * XCOLS + 2 * B * OUT_C * LOCS + 4 * LOCS * OUT_C * XCOLS
+
+LOC_ORDER = (4, 3, 5, 1, 0, 2, 7, 6, 8)
+GROUP_ORDER = (1, 0, 2)
+
+
+def valid(loc):
+    return max(0, loc - 1), min(SIDE, loc + 2)
+
+
+def tile_locallyconnected2d_kernel(tc, x, weights, bias, grad_out, out):
+    nc = tc.nc
+    with ExitStack() as stack:
+        keep = stack.enter_context(tc.tile_pool(name="keep", bufs=1))
+        outs = stack.enter_context(tc.tile_pool(name="outs", bufs=8))
+        psum = stack.enter_context(tc.psum_pool(name="psum", bufs=8))
+
+        x_raw = keep.tile([P, PACK, XCOLS], BF16, name="x_raw")
+        x_grp = keep.tile([P, XCOLS, PACK], BF16, name="x_grp", align_bytes=64)
+        x_scales = keep.tile([P, XWIDE], U8, name="x_scales", align_bytes=64)
+        x_codes = {}
+        for loc in range(LOCS):
+            x_codes[loc] = keep.tile([P, XWIDE], I32, name="x_codes%d" % loc, align_bytes=64)
+        g_raw, g_grp, g_codes, g_scales = {}, {}, {}, {}
+        for t in range(O_TILES):
+            g_raw[t] = keep.tile([P, PACK, XCOLS], BF16, name="g_raw%d" % t)
+            g_grp[t] = keep.tile([P, LOCS, P, PACK], BF16, name="g_grp%d" % t, align_bytes=64)
+            g_codes[t] = keep.tile([P, LOCS * P], I32, name="g_codes%d" % t, align_bytes=64)
+            g_scales[t] = keep.tile([P, LOCS * P], U8, name="g_scales%d" % t, align_bytes=64)
+
+        nc.sync.dma_start(out=x_raw[:], in_=x.rearrange("(p j) c h w -> p j (c h w)", j=PACK))
+        g_rows = grad_out.rearrange("(p j) o h w -> p j (o h w)", j=PACK)
+        for t in range(O_TILES):
+            nc.sync.dma_start(out=g_raw[t][:], in_=g_rows[:, :, t * XCOLS : (t + 1) * XCOLS])
+
+        nc.vector.memset(x_scales[:].bitcast(I32), 0)
+        nc.vector.memset(x_codes[4][:, 0:PAD], 0)
+        nc.vector.memset(x_codes[4][:, PAD + XCOLS : XWIDE], 0)
+        for n, loc in enumerate(LOC_ORDER[1:]):
+            if n < 4:
+                nc.vector.memset(x_codes[loc][:], 0)
+            else:
+                nc.gpsimd.memset(x_codes[loc][:], 0)
+
+        def regroup_x(engine_copy, c0, c1):
+            engine_copy(
+                out=x_grp[:, c0:c1, :].rearrange("p (c i) t -> p c t i", i=4),
+                in_=x_raw[:, :, c0:c1].rearrange("p t (c i) -> p c t i", i=4),
+            )
+
+        regroup_x(nc.vector.tensor_copy, 0, 768)
+        regroup_x(nc.scalar.copy, 768, XCOLS)
+        x_flat = x_grp[:].rearrange("p c t -> p (c t)")
+        for c0, c1 in ((0, 1024), (1024, XCOLS)):
+            nc.vector.quantize_mx(
+                out=x_codes[4][:, PAD + c0 : PAD + c1].bitcast(E4X4),
+                scales=x_scales[:, PAD + c0 : PAD + c1],
+                in_=x_flat[:, PACK * c0 : PACK * c1],
+            )
+
+        def prepare_g(t, a, engine_copy):
+            engine_copy(
+                out=g_grp[t][:, GROUP * a : GROUP * (a + 1), :, :].rearrange("p e o j -> p o j e"),
+                in_=g_raw[t][:].rearrange("p j (o q) -> p o j q", q=LOCS)[:, :, :, GROUP * a : GROUP * (a + 1)],
+            )
+            flat = g_grp[t][:].rearrange("p q o j -> p (q o j)")
+            base = GROUP * a * P
+            for c0, c1 in ((base, base + 256), (base + 256, base + 384)):
+                nc.vector.quantize_mx(
+                    out=g_codes[t][:, c0:c1].bitcast(E5X4),
+                    scales=g_scales[t][:, c0:c1],
+                    in_=flat[:, PACK * c0 : PACK * c1],
+                )
+
+        def mask_x(loc):
+            y0, y1 = valid(loc // SIDE)
+            v0, v1 = valid(loc % SIDE)
+            nc.vector.tensor_copy(
+                out=x_codes[loc][:, PAD : PAD + XCOLS].rearrange("p (c y v) -> p c y v", y=SIDE, v=SIDE)[:, :, y0:y1, v0:v1],
+                in_=x_codes[4][:, PAD : PAD + XCOLS].rearrange("p (c y v) -> p c y v", y=SIDE, v=SIDE)[:, :, y0:y1, v0:v1],
+            )
+
+        count = [0]
+
+        def produce(t, loc):
+            h, w = loc // SIDE, loc % SIDE
+            shift = SIDE * (h - 1) + (w - 1)
+            res = outs.tile([P, XCOLS], F32, name="res")
+            for part in range(3):
+                acc = psum.tile([P, WIN], F32, name="acc")
+                nc.tensor.matmul_mx(
+                    out=acc[:],
+                    lhsT=g_codes[t][:, loc * P : (loc + 1) * P].bitcast(E5X4),
+                    lhsT_scale=g_scales[t][:, loc * P : (loc + 1) * P],
+                    rhs=x_codes[loc][:, part * STEP : part * STEP + WIN].bitcast(E4X4),
+                    rhs_scale=x_scales[:, part * STEP : part * STEP + WIN],
+                    start=True,
+                    stop=True,
+                )
+                src = acc[:, PAD + shift : PAD + shift + STEP]
+                dst = res[:, part * STEP : (part + 1) * STEP]
+                if t > 0 and count[0] % 2 == 0:
+                    nc.vector.tensor_copy(out=dst, in_=src)
+                else:
+                    nc.scalar.copy(out=dst, in_=src)
+                count[0] += 1
+            nc.sync.dma_start(
+                out=out[h, w, t * P : (t + 1) * P].rearrange("o c i j -> o (c i j)"), in_=res[:]
+            )
+
+        copies = (nc.vector.tensor_copy, nc.scalar.copy, nc.vector.tensor_copy)
+        for n, a in enumerate(GROUP_ORDER):
+            prepare_g(0, a, copies[n])
+        for t in range(O_TILES):
+            for n, loc in enumerate(LOC_ORDER):
+                if t == 0 and loc != 4:
+                    mask_x(loc)
+                produce(t, loc)
+                if t + 1 < O_TILES and n % 3 == 1:
+                    prepare_g(t + 1, GROUP_ORDER[n // 3], copies[n // 3])

@@ -24,8 +24,10 @@ GROUP = 3
 FLOPS = 2 * 49 * OUT_C * IN_C * B
 BYTES = 2 * B * XCOLS + 2 * B * OUT_C * LOCS + 4 * LOCS * OUT_C * XCOLS
 
-LOC_ORDER = (4, 3, 5, 1, 0, 2, 7, 6, 8)
-GROUP_ORDER = (1, 0, 2)
+PINNED = False
+V_EVERY = 5
+V_FROM = 0
+RES_BUFS = 6
 
 
 def valid(loc):
@@ -36,8 +38,10 @@ def tile_locallyconnected2d_kernel(tc, x, weights, bias, grad_out, out):
     nc = tc.nc
     with ExitStack() as stack:
         keep = stack.enter_context(tc.tile_pool(name="keep", bufs=1))
-        outs = stack.enter_context(tc.tile_pool(name="outs", bufs=8))
+        outs = stack.enter_context(tc.tile_pool(name="outs", bufs=RES_BUFS))
         psum = stack.enter_context(tc.psum_pool(name="psum", bufs=8))
+        if PINNED:
+            stack.enter_context(tc.manual_schedule())
 
         x_raw = keep.tile([P, PACK, XCOLS], BF16, name="x_raw")
         x_grp = keep.tile([P, XCOLS, PACK], BF16, name="x_grp", align_bytes=64)
@@ -45,26 +49,33 @@ def tile_locallyconnected2d_kernel(tc, x, weights, bias, grad_out, out):
         x_codes = {}
         for loc in range(LOCS):
             x_codes[loc] = keep.tile([P, XWIDE], I32, name="x_codes%d" % loc, align_bytes=64)
-        g_raw, g_grp, g_codes, g_scales = {}, {}, {}, {}
+        g_raw = {}
         for t in range(O_TILES):
             g_raw[t] = keep.tile([P, PACK, XCOLS], BF16, name="g_raw%d" % t)
-            g_grp[t] = keep.tile([P, LOCS, P, PACK], BF16, name="g_grp%d" % t, align_bytes=64)
-            g_codes[t] = keep.tile([P, LOCS * P], I32, name="g_codes%d" % t, align_bytes=64)
-            g_scales[t] = keep.tile([P, LOCS * P], U8, name="g_scales%d" % t, align_bytes=64)
+        m_grp, m_codes, m_scales = {}, {}, {}
+        for t in range(O_TILES):
+            m_grp[t] = keep.tile([P, GROUP, P, PACK], BF16, name="m_grp%d" % t, align_bytes=64)
+            m_codes[t] = keep.tile([P, GROUP * P], I32, name="m_codes%d" % t, align_bytes=64)
+            m_scales[t] = keep.tile([P, GROUP * P], U8, name="m_scales%d" % t, align_bytes=64)
+        r_grp, r_codes, r_scales = {}, {}, {}
+        for a in (0, 2):
+            r_grp[a] = keep.tile([P, GROUP, O_TILES, P, PACK], BF16, name="r_grp%d" % a, align_bytes=64)
+            r_codes[a] = keep.tile([P, GROUP * OUT_C], I32, name="r_codes%d" % a, align_bytes=64)
+            r_scales[a] = keep.tile([P, GROUP * OUT_C], U8, name="r_scales%d" % a, align_bytes=64)
 
         nc.sync.dma_start(out=x_raw[:], in_=x.rearrange("(p j) c h w -> p j (c h w)", j=PACK))
         g_rows = grad_out.rearrange("(p j) o h w -> p j (o h w)", j=PACK)
         for t in range(O_TILES):
-            nc.sync.dma_start(out=g_raw[t][:], in_=g_rows[:, :, t * XCOLS : (t + 1) * XCOLS])
+            cols = slice(t * XCOLS, (t + 1) * XCOLS)
+            nc.sync.dma_start(out=g_raw[t][:], in_=g_rows[:, :, cols])
 
         nc.vector.memset(x_scales[:].bitcast(I32), 0)
         nc.vector.memset(x_codes[4][:, 0:PAD], 0)
         nc.vector.memset(x_codes[4][:, PAD + XCOLS : XWIDE], 0)
-        for n, loc in enumerate(LOC_ORDER[1:]):
-            if n < 4:
-                nc.vector.memset(x_codes[loc][:], 0)
-            else:
-                nc.gpsimd.memset(x_codes[loc][:], 0)
+        for loc in (3, 5, 1, 0):
+            nc.vector.memset(x_codes[loc][:], 0)
+        for loc in (2, 7, 6, 8):
+            nc.gpsimd.memset(x_codes[loc][:], 0)
 
         def regroup_x(engine_copy, c0, c1):
             engine_copy(
@@ -82,19 +93,33 @@ def tile_locallyconnected2d_kernel(tc, x, weights, bias, grad_out, out):
                 in_=x_flat[:, PACK * c0 : PACK * c1],
             )
 
-        def prepare_g(t, a, engine_copy):
-            engine_copy(
-                out=g_grp[t][:, GROUP * a : GROUP * (a + 1), :, :].rearrange("p e o j -> p o j e"),
-                in_=g_raw[t][:].rearrange("p j (o q) -> p o j q", q=LOCS)[:, :, :, GROUP * a : GROUP * (a + 1)],
+        def quantise_g(codes, scales, flat, c0, c1):
+            nc.vector.quantize_mx(
+                out=codes[:, c0:c1].bitcast(E5X4), scales=scales[:, c0:c1], in_=flat[:, PACK * c0 : PACK * c1]
             )
-            flat = g_grp[t][:].rearrange("p q o j -> p (q o j)")
-            base = GROUP * a * P
-            for c0, c1 in ((base, base + 256), (base + 256, base + 384)):
-                nc.vector.quantize_mx(
-                    out=g_codes[t][:, c0:c1].bitcast(E5X4),
-                    scales=g_scales[t][:, c0:c1],
-                    in_=flat[:, PACK * c0 : PACK * c1],
-                )
+
+        def prepare_middle(t):
+            nc.vector.tensor_copy(
+                out=m_grp[t][:].rearrange("p e o j -> p o j e"),
+                in_=g_raw[t][:].rearrange("p j (o q) -> p o j q", q=LOCS)[
+                    :, :, :, GROUP : 2 * GROUP
+                ],
+            )
+            flat = m_grp[t][:].rearrange("p e o j -> p (e o j)")
+            quantise_g(m_codes[t], m_scales[t], flat, 0, 256)
+            quantise_g(m_codes[t], m_scales[t], flat, 256, 384)
+
+        def regroup_row(a, t):
+            nc.vector.tensor_copy(
+                out=r_grp[a][:, :, :, 32 * t : 32 * (t + 1), :].rearrange("p e r o j -> p r o j e"),
+                in_=g_raw[t][:].rearrange("p j (o r q) -> p r o j q", r=O_TILES, q=LOCS)[
+                    :, :, :, :, GROUP * a : GROUP * (a + 1)
+                ],
+            )
+
+        def quantise_row(a, e):
+            flat = r_grp[a][:].rearrange("p e r o j -> p (e r o j)")
+            quantise_g(r_codes[a], r_scales[a], flat, e * OUT_C, (e + 1) * OUT_C)
 
         def mask_x(loc):
             y0, y1 = valid(loc // SIDE)
@@ -106,39 +131,68 @@ def tile_locallyconnected2d_kernel(tc, x, weights, bias, grad_out, out):
 
         count = [0]
 
-        def produce(t, loc):
-            h, w = loc // SIDE, loc % SIDE
-            shift = SIDE * (h - 1) + (w - 1)
-            res = outs.tile([P, XCOLS], F32, name="res")
+        def product(loc, lhs, lhs_scale, dst_row):
+            shift = SIDE * (loc // SIDE - 1) + (loc % SIDE - 1)
             for part in range(3):
                 acc = psum.tile([P, WIN], F32, name="acc")
                 nc.tensor.matmul_mx(
                     out=acc[:],
-                    lhsT=g_codes[t][:, loc * P : (loc + 1) * P].bitcast(E5X4),
-                    lhsT_scale=g_scales[t][:, loc * P : (loc + 1) * P],
+                    lhsT=lhs.bitcast(E5X4),
+                    lhsT_scale=lhs_scale,
                     rhs=x_codes[loc][:, part * STEP : part * STEP + WIN].bitcast(E4X4),
                     rhs_scale=x_scales[:, part * STEP : part * STEP + WIN],
                     start=True,
                     stop=True,
                 )
                 src = acc[:, PAD + shift : PAD + shift + STEP]
-                dst = res[:, part * STEP : (part + 1) * STEP]
-                if t > 0 and count[0] % 2 == 0:
+                dst = dst_row[:, part * STEP : (part + 1) * STEP]
+                k = count[0]
+                if k >= V_FROM and k % V_EVERY == 0:
                     nc.vector.tensor_copy(out=dst, in_=src)
                 else:
                     nc.scalar.copy(out=dst, in_=src)
                 count[0] += 1
-            nc.sync.dma_start(
-                out=out[h, w, t * P : (t + 1) * P].rearrange("o c i j -> o (c i j)"), in_=res[:]
-            )
 
-        copies = (nc.vector.tensor_copy, nc.scalar.copy, nc.vector.tensor_copy)
-        for n, a in enumerate(GROUP_ORDER):
-            prepare_g(0, a, copies[n])
+        res_of = {}
+        prepare_middle(0)
+        extra = {0: [lambda: mask_x(1), lambda: mask_x(0)], 1: [lambda: mask_x(2)], 2: [], 3: []}
         for t in range(O_TILES):
-            for n, loc in enumerate(LOC_ORDER):
+            for loc in (4, 3, 5):
                 if t == 0 and loc != 4:
                     mask_x(loc)
-                produce(t, loc)
-                if t + 1 < O_TILES and n % 3 == 1:
-                    prepare_g(t + 1, GROUP_ORDER[n // 3], copies[n // 3])
+                if t % 2 == 0:
+                    res_of[loc] = outs.tile([P, 2, XCOLS], F32, name="res")
+                res = res_of[loc]
+                cols = slice((loc - GROUP) * P, (loc - GROUP + 1) * P)
+                product(loc, m_codes[t][:, cols], m_scales[t][:, cols], res[:, t % 2, :])
+                nc.sync.dma_start(
+                    out=out[loc // SIDE, loc % SIDE, t * P : (t + 1) * P].rearrange("o c i j -> o (c i j)"),
+                    in_=res[:, t % 2, :],
+                )
+            if t + 1 < O_TILES:
+                prepare_middle(t + 1)
+            for job in extra[t]:
+                job()
+
+        def prepare_row(a):
+            for r in range(O_TILES):
+                regroup_row(a, r)
+            for e in range(GROUP):
+                quantise_row(a, e)
+
+        prepare_row(0)
+        for a in (0, 2):
+            for e, loc in enumerate((GROUP * a + 1, GROUP * a, GROUP * a + 2)):
+                el = loc - GROUP * a
+                if a == 2:
+                    mask_x(loc)
+                view = out[loc // SIDE, loc % SIDE].rearrange("(p r) c i j -> p r (c i j)", r=O_TILES)
+                for half in range(2):
+                    res = outs.tile([P, 2, XCOLS], F32, name="res")
+                    for s in range(2):
+                        r = 2 * half + s
+                        cols = slice(el * OUT_C + r * P, el * OUT_C + (r + 1) * P)
+                        product(loc, r_codes[a][:, cols], r_scales[a][:, cols], res[:, s, :])
+                    nc.sync.dma_start(out=view[:, 2 * half : 2 * half + 2, :], in_=res[:])
+                if a == 0 and e == 0:
+                    prepare_row(2)

@@ -75,7 +75,7 @@ def tile_locallyconnected2d_kernel(tc, x, weights, bias, grad_out, out):
         for loc in (3, 5, 1, 0):
             nc.vector.memset(x_codes[loc][:], 0)
         for loc in (2, 7, 6, 8):
-            nc.gpsimd.memset(x_codes[loc][:], 0)
+            nc.gpsimd.memset(x_codes[loc][:].bitcast(F32), 0.0)
 
         def regroup_x(engine_copy, c0, c1):
             engine_copy(

@@ -25,7 +25,7 @@ FLOPS = 2 * 49 * OUT_C * IN_C * B
 BYTES = 2 * B * XCOLS + 2 * B * OUT_C * LOCS + 4 * LOCS * OUT_C * XCOLS
 
 PINNED = False
-V_EVERY = 5
+V_EVERY = 9
 V_FROM = 0
 RES_BUFS = 6
 

@@ -20,13 +20,12 @@ WIN = 512
 STEP = 384
 XWIDE = 2 * STEP + WIN
 GROUP = 3
+UNITS = 8
 
 FLOPS = 2 * 49 * OUT_C * IN_C * B
 BYTES = 2 * B * XCOLS + 2 * B * OUT_C * LOCS + 4 * LOCS * OUT_C * XCOLS
 
-PINNED = False
-V_EVERY = 9
-V_FROM = 0
+V_SHARE = (9, 9, 9, 9, 6, 6, 3, 2)
 RES_BUFS = 6
 
 
@@ -40,8 +39,6 @@ def tile_locallyconnected2d_kernel(tc, x, weights, bias, grad_out, out):
         keep = stack.enter_context(tc.tile_pool(name="keep", bufs=1))
         outs = stack.enter_context(tc.tile_pool(name="outs", bufs=RES_BUFS))
         psum = stack.enter_context(tc.psum_pool(name="psum", bufs=8))
-        if PINNED:
-            stack.enter_context(tc.manual_schedule())
 
         x_raw = keep.tile([P, PACK, XCOLS], BF16, name="x_raw")
         x_grp = keep.tile([P, XCOLS, PACK], BF16, name="x_grp", align_bytes=64)
@@ -52,16 +49,12 @@ def tile_locallyconnected2d_kernel(tc, x, weights, bias, grad_out, out):
         g_raw = {}
         for t in range(O_TILES):
             g_raw[t] = keep.tile([P, PACK, XCOLS], BF16, name="g_raw%d" % t)
-        m_grp, m_codes, m_scales = {}, {}, {}
-        for t in range(O_TILES):
-            m_grp[t] = keep.tile([P, GROUP, P, PACK], BF16, name="m_grp%d" % t, align_bytes=64)
-            m_codes[t] = keep.tile([P, GROUP * P], I32, name="m_codes%d" % t, align_bytes=64)
-            m_scales[t] = keep.tile([P, GROUP * P], U8, name="m_scales%d" % t, align_bytes=64)
-        r_grp, r_codes, r_scales = {}, {}, {}
-        for a in (0, 2):
-            r_grp[a] = keep.tile([P, GROUP, O_TILES, P, PACK], BF16, name="r_grp%d" % a, align_bytes=64)
-            r_codes[a] = keep.tile([P, GROUP * OUT_C], I32, name="r_codes%d" % a, align_bytes=64)
-            r_scales[a] = keep.tile([P, GROUP * OUT_C], U8, name="r_scales%d" % a, align_bytes=64)
+        g_grp, g_codes, g_scales = {}, {}, {}
+        for n in range(UNITS):
+            width = GROUP * P if n < O_TILES else GROUP * 2 * P
+            g_grp[n] = keep.tile([P, width * PACK], BF16, name="g_grp%d" % n, align_bytes=64)
+            g_codes[n] = keep.tile([P, width], I32, name="g_codes%d" % n, align_bytes=64)
+            g_scales[n] = keep.tile([P, width], U8, name="g_scales%d" % n, align_bytes=64)
 
         nc.sync.dma_start(out=x_raw[:], in_=x.rearrange("(p j) c h w -> p j (c h w)", j=PACK))
         g_rows = grad_out.rearrange("(p j) o h w -> p j (o h w)", j=PACK)
@@ -72,9 +65,9 @@ def tile_locallyconnected2d_kernel(tc, x, weights, bias, grad_out, out):
         nc.vector.memset(x_scales[:].bitcast(I32), 0)
         nc.vector.memset(x_codes[4][:, 0:PAD], 0)
         nc.vector.memset(x_codes[4][:, PAD + XCOLS : XWIDE], 0)
-        for loc in (3, 5, 1, 0):
+        for loc in (3, 5, 0, 1):
             nc.vector.memset(x_codes[loc][:], 0)
-        for loc in (2, 7, 6, 8):
+        for loc in (2, 6, 7, 8):
             nc.gpsimd.memset(x_codes[loc][:].bitcast(F32), 0.0)
 
         def regroup_x(engine_copy, c0, c1):
@@ -83,62 +76,78 @@ def tile_locallyconnected2d_kernel(tc, x, weights, bias, grad_out, out):
                 in_=x_raw[:, :, c0:c1].rearrange("p t (c i) -> p c t i", i=4),
             )
 
-        regroup_x(nc.vector.tensor_copy, 0, 768)
-        regroup_x(nc.scalar.copy, 768, XCOLS)
         x_flat = x_grp[:].rearrange("p c t -> p (c t)")
-        for c0, c1 in ((0, 1024), (1024, XCOLS)):
+
+        def quantise_x(c0, c1):
             nc.vector.quantize_mx(
                 out=x_codes[4][:, PAD + c0 : PAD + c1].bitcast(E4X4),
                 scales=x_scales[:, PAD + c0 : PAD + c1],
                 in_=x_flat[:, PACK * c0 : PACK * c1],
             )
 
-        def quantise_g(codes, scales, flat, c0, c1):
-            nc.vector.quantize_mx(
-                out=codes[:, c0:c1].bitcast(E5X4), scales=scales[:, c0:c1], in_=flat[:, PACK * c0 : PACK * c1]
-            )
+        def row_of(n):
+            return 1 if n < O_TILES else (0 if n < O_TILES + 2 else 2)
 
-        def prepare_middle(t):
-            nc.vector.tensor_copy(
-                out=m_grp[t][:].rearrange("p e o j -> p o j e"),
-                in_=g_raw[t][:].rearrange("p j (o q) -> p o j q", q=LOCS)[
-                    :, :, :, GROUP : 2 * GROUP
-                ],
-            )
-            flat = m_grp[t][:].rearrange("p e o j -> p (e o j)")
-            quantise_g(m_codes[t], m_scales[t], flat, 0, 256)
-            quantise_g(m_codes[t], m_scales[t], flat, 256, 384)
+        def regroup_jobs(n):
+            a = row_of(n)
+            if n < O_TILES:
+                def middle():
+                    nc.vector.tensor_copy(
+                        out=g_grp[n][:].rearrange("p (l o j) -> p o j l", l=GROUP, j=PACK),
+                        in_=g_raw[n][:].rearrange("p j (o q) -> p o j q", q=LOCS)[:, :, :, GROUP * a : GROUP * (a + 1)],
+                    )
+                return [middle]
+            u = (n - O_TILES) % 2
 
-        def regroup_row(a, t):
-            nc.vector.tensor_copy(
-                out=r_grp[a][:, :, :, 32 * t : 32 * (t + 1), :].rearrange("p e r o j -> p r o j e"),
-                in_=g_raw[t][:].rearrange("p j (o r q) -> p r o j q", r=O_TILES, q=LOCS)[
-                    :, :, :, :, GROUP * a : GROUP * (a + 1)
-                ],
-            )
+            def half(s):
+                def job():
+                    nc.vector.tensor_copy(
+                        out=g_grp[n][:].rearrange("p (l e o j) -> p e o j l", l=GROUP, e=2, j=PACK)[
+                            :, :, 64 * s : 64 * (s + 1), :, :
+                        ],
+                        in_=g_raw[2 * u + s][:].rearrange("p j (o e q) -> p e o j q", e=2, q=LOCS)[
+                            :, :, :, :, GROUP * a : GROUP * (a + 1)
+                        ],
+                    )
+                return job
 
-        def quantise_row(a, e):
-            flat = r_grp[a][:].rearrange("p e r o j -> p (e r o j)")
-            quantise_g(r_codes[a], r_scales[a], flat, e * OUT_C, (e + 1) * OUT_C)
+            return [half(0), half(1)]
 
-        def mask_x(loc):
-            y0, y1 = valid(loc // SIDE)
-            v0, v1 = valid(loc % SIDE)
-            nc.vector.tensor_copy(
-                out=x_codes[loc][:, PAD : PAD + XCOLS].rearrange("p (c y v) -> p c y v", y=SIDE, v=SIDE)[:, :, y0:y1, v0:v1],
-                in_=x_codes[4][:, PAD : PAD + XCOLS].rearrange("p (c y v) -> p c y v", y=SIDE, v=SIDE)[:, :, y0:y1, v0:v1],
-            )
+        def quantise_jobs(n):
+            cuts = (0, 256, 384) if n < O_TILES else (0, 512, 768)
+
+            def part(c0, c1):
+                def job():
+                    nc.vector.quantize_mx(
+                        out=g_codes[n][:, c0:c1].bitcast(E5X4),
+                        scales=g_scales[n][:, c0:c1],
+                        in_=g_grp[n][:, PACK * c0 : PACK * c1],
+                    )
+                return job
+
+            return [part(cuts[0], cuts[1]), part(cuts[1], cuts[2])]
+
+        def mask_job(loc):
+            def job():
+                y0, y1 = valid(loc // SIDE)
+                v0, v1 = valid(loc % SIDE)
+                nc.vector.tensor_copy(
+                    out=x_codes[loc][:, PAD : PAD + XCOLS].rearrange("p (c y v) -> p c y v", y=SIDE, v=SIDE)[:, :, y0:y1, v0:v1],
+                    in_=x_codes[4][:, PAD : PAD + XCOLS].rearrange("p (c y v) -> p c y v", y=SIDE, v=SIDE)[:, :, y0:y1, v0:v1],
+                )
+            return job
 
         count = [0]
 
-        def product(loc, lhs, lhs_scale, dst_row):
+        def product(loc, n, col0, dst_row):
             shift = SIDE * (loc // SIDE - 1) + (loc % SIDE - 1)
+            every = V_SHARE[n]
             for part in range(3):
                 acc = psum.tile([P, WIN], F32, name="acc")
                 nc.tensor.matmul_mx(
                     out=acc[:],
-                    lhsT=lhs.bitcast(E5X4),
-                    lhsT_scale=lhs_scale,
+                    lhsT=g_codes[n][:, col0 : col0 + P].bitcast(E5X4),
+                    lhsT_scale=g_scales[n][:, col0 : col0 + P],
                     rhs=x_codes[loc][:, part * STEP : part * STEP + WIN].bitcast(E4X4),
                     rhs_scale=x_scales[:, part * STEP : part * STEP + WIN],
                     start=True,
@@ -146,53 +155,69 @@ def tile_locallyconnected2d_kernel(tc, x, weights, bias, grad_out, out):
                 )
                 src = acc[:, PAD + shift : PAD + shift + STEP]
                 dst = dst_row[:, part * STEP : (part + 1) * STEP]
-                k = count[0]
-                if k >= V_FROM and k % V_EVERY == 0:
+                if count[0] % every == every - 1:
                     nc.vector.tensor_copy(out=dst, in_=src)
                 else:
                     nc.scalar.copy(out=dst, in_=src)
                 count[0] += 1
 
+        regroup_x(nc.vector.tensor_copy, 0, 512)
+        regroup_x(nc.scalar.copy, 512, XCOLS)
+        quantise_x(0, 512)
+        regroup_jobs(0)[0]()
+        quantise_jobs(0)[0]()
+        quantise_x(512, 1024)
+        quantise_x(1024, XCOLS)
+        quantise_jobs(0)[1]()
+
+        def plan(n):
+            r = regroup_jobs(n + 1) if n + 1 < UNITS else []
+            q = quantise_jobs(n + 1) if n + 1 < UNITS else []
+            first_row = regroup_jobs(O_TILES)
+            if n == 0:
+                return [mask_job(3), r[0], mask_job(5), q[0], q[1]]
+            if n == 1:
+                return [r[0], first_row[0], q[0], q[1]]
+            if n == 2:
+                return [r[0], first_row[1], q[0], q[1]]
+            if n == 3:
+                return [mask_job(0), q[0], mask_job(1), q[1]]
+            if n == 4:
+                return [mask_job(2), r[0], r[1], mask_job(6), q[0], q[1]]
+            if n == 5:
+                return [r[0], r[1], mask_job(7), q[0], q[1], mask_job(8)]
+            return r + q
+
         res_of = {}
-        prepare_middle(0)
-        extra = {0: [lambda: mask_x(1), lambda: mask_x(0)], 1: [lambda: mask_x(2)], 2: [], 3: []}
-        for t in range(O_TILES):
-            for loc in (4, 3, 5):
-                if t == 0 and loc != 4:
-                    mask_x(loc)
-                if t % 2 == 0:
-                    res_of[loc] = outs.tile([P, 2, XCOLS], F32, name="res")
-                res = res_of[loc]
-                cols = slice((loc - GROUP) * P, (loc - GROUP + 1) * P)
-                product(loc, m_codes[t][:, cols], m_scales[t][:, cols], res[:, t % 2, :])
-                nc.sync.dma_start(
-                    out=out[loc // SIDE, loc % SIDE, t * P : (t + 1) * P].rearrange("o c i j -> o (c i j)"),
-                    in_=res[:, t % 2, :],
-                )
-            if t + 1 < O_TILES:
-                prepare_middle(t + 1)
-            for job in extra[t]:
-                job()
-
-        def prepare_row(a):
-            for r in range(O_TILES):
-                regroup_row(a, r)
-            for e in range(GROUP):
-                quantise_row(a, e)
-
-        prepare_row(0)
-        for a in (0, 2):
-            for e, loc in enumerate((GROUP * a + 1, GROUP * a, GROUP * a + 2)):
+        for n in range(UNITS):
+            jobs = plan(n)
+            a = row_of(n)
+            if n < O_TILES:
+                products = [(4, 0), (3, 0), (5, 0)]
+            else:
+                products = [(GROUP * a + el, e) for el in range(GROUP) for e in range(2)]
+            issued = 0
+            for k, (loc, e) in enumerate(products):
                 el = loc - GROUP * a
-                if a == 2:
-                    mask_x(loc)
-                view = out[loc // SIDE, loc % SIDE].rearrange("(p r) c i j -> p r (c i j)", r=O_TILES)
-                for half in range(2):
-                    res = outs.tile([P, 2, XCOLS], F32, name="res")
-                    for s in range(2):
-                        r = 2 * half + s
-                        cols = slice(el * OUT_C + r * P, el * OUT_C + (r + 1) * P)
-                        product(loc, r_codes[a][:, cols], r_scales[a][:, cols], res[:, s, :])
-                    nc.sync.dma_start(out=view[:, 2 * half : 2 * half + 2, :], in_=res[:])
-                if a == 0 and e == 0:
-                    prepare_row(2)
+                if n < O_TILES:
+                    if n % 2 == 0:
+                        res_of[loc] = outs.tile([P, 2, XCOLS], F32, name="res")
+                    res = res_of[loc]
+                    product(loc, n, el * P, res[:, n % 2, :])
+                    nc.sync.dma_start(
+                        out=out[loc // SIDE, loc % SIDE, n * P : (n + 1) * P].rearrange("o c i j -> o (c i j)"),
+                        in_=res[:, n % 2, :],
+                    )
+                else:
+                    u = (n - O_TILES) % 2
+                    if e == 0:
+                        res_of[loc] = outs.tile([P, 2, XCOLS], F32, name="res")
+                    res = res_of[loc]
+                    product(loc, n, (2 * el + e) * P, res[:, e, :])
+                    if e == 1:
+                        view = out[loc // SIDE, loc % SIDE].rearrange("(u p e) c i j -> u p e (c i j)", u=2, e=2)
+                        nc.sync.dma_start(out=view[u], in_=res[:])
+                want = ((k + 1) * len(jobs) + len(products) - 1) // len(products)
+                while issued < want:
+                    jobs[issued]()
+                    issued += 1

@@ -39,6 +39,7 @@ def tile_locallyconnected2d_kernel(tc, x, weights, bias, grad_out, out):
         keep = stack.enter_context(tc.tile_pool(name="keep", bufs=1))
         outs = stack.enter_context(tc.tile_pool(name="outs", bufs=RES_BUFS))
         psum = stack.enter_context(tc.psum_pool(name="psum", bufs=8))
+        stack.enter_context(tc.manual_schedule())
 
         x_raw = keep.tile([P, PACK, XCOLS], BF16, name="x_raw")
         x_grp = keep.tile([P, XCOLS, PACK], BF16, name="x_grp", align_bytes=64)

@@ -25,7 +25,7 @@ UNITS = 8
 FLOPS = 2 * 49 * OUT_C * IN_C * B
 BYTES = 2 * B * XCOLS + 2 * B * OUT_C * LOCS + 4 * LOCS * OUT_C * XCOLS
 
-V_SHARE = (9, 9, 9, 9, 6, 6, 3, 2)
+V_SHARE = (18, 18, 18, 18, 6, 6, 3, 2)
 RES_BUFS = 6
 
 
@@ -176,7 +176,7 @@ def tile_locallyconnected2d_kernel(tc, x, weights, bias, grad_out, out):
             q = quantise_jobs(n + 1) if n + 1 < UNITS else []
             first_row = regroup_jobs(O_TILES)
             if n == 0:
-                return [mask_job(3), r[0], mask_job(5), q[0], q[1]]
+                return [mask_job(3), mask_job(5), r[0], q[0], q[1]]
             if n == 1:
                 return [r[0], first_row[0], q[0], q[1]]
             if n == 2:

@@ -45,8 +45,10 @@ def tile_locallyconnected2d_kernel(tc, x, weights, bias, grad_out, out):
         x_grp = keep.tile([P, XCOLS, PACK], BF16, name="x_grp", align_bytes=64)
         x_scales = keep.tile([P, XWIDE], U8, name="x_scales", align_bytes=64)
         x_codes = {}
-        for loc in range(LOCS):
+        for loc in range(2 * SIDE):
             x_codes[loc] = keep.tile([P, XWIDE], I32, name="x_codes%d" % loc, align_bytes=64)
+        for loc in range(2 * SIDE, LOCS):
+            x_codes[loc] = x_codes[loc - 2 * SIDE]
         g_raw = {}
         for t in range(O_TILES):
             g_raw[t] = keep.tile([P, PACK, XCOLS], BF16, name="g_raw%d" % t)
@@ -63,13 +65,12 @@ def tile_locallyconnected2d_kernel(tc, x, weights, bias, grad_out, out):
             cols = slice(t * XCOLS, (t + 1) * XCOLS)
             nc.sync.dma_start(out=g_raw[t][:], in_=g_rows[:, :, cols])
 
-        nc.vector.memset(x_scales[:].bitcast(I32), 0)
-        nc.vector.memset(x_codes[4][:, 0:PAD], 0)
-        nc.vector.memset(x_codes[4][:, PAD + XCOLS : XWIDE], 0)
+        nc.gpsimd.memset(x_scales[:].bitcast(F32), 0.0)
+        nc.gpsimd.memset(x_codes[4][:, 0:PAD].bitcast(F32), 0.0)
+        nc.gpsimd.memset(x_codes[4][:, PAD + XCOLS : XWIDE].bitcast(F32), 0.0)
         for loc in (3, 5, 0, 1):
-            nc.vector.memset(x_codes[loc][:], 0)
-        for loc in (2, 6, 7, 8):
             nc.gpsimd.memset(x_codes[loc][:].bitcast(F32), 0.0)
+        nc.vector.memset(x_codes[2][:], 0)
 
         def regroup_x(engine_copy, c0, c1):
             engine_copy(
@@ -138,6 +139,22 @@ def tile_locallyconnected2d_kernel(tc, x, weights, bias, grad_out, out):
                 )
             return job
 
+        def taps(tile, y0, y1, v0, v1):
+            return tile[:, PAD : PAD + XCOLS].rearrange("p (c y v) -> p c y v", y=SIDE, v=SIDE)[:, :, y0:y1, v0:v1]
+
+        def turn_job(loc):
+            def job():
+                v0, v1 = valid(loc % SIDE)
+                nc.vector.memset(taps(x_codes[loc], 0, 1, v0, v1), 0)
+                nc.vector.tensor_copy(out=taps(x_codes[loc], 2, 3, v0, v1), in_=taps(x_codes[4], 2, 3, v0, v1))
+            return job
+
+        def both(first, second):
+            def job():
+                first()
+                second()
+            return job
+
         count = [0]
 
         def product(loc, n, col0, dst_row):
@@ -184,9 +201,9 @@ def tile_locallyconnected2d_kernel(tc, x, weights, bias, grad_out, out):
             if n == 3:
                 return [mask_job(0), q[0], mask_job(1), q[1]]
             if n == 4:
-                return [mask_job(2), r[0], r[1], mask_job(6), q[0], q[1]]
+                return [mask_job(2), r[0], r[1], q[0], q[1]]
             if n == 5:
-                return [r[0], r[1], mask_job(7), q[0], q[1], mask_job(8)]
+                return [r[0], turn_job(6), r[1], turn_job(7), both(q[0], q[1]), turn_job(8)]
             return r + q
 
         res_of = {}

@@ -45,10 +45,11 @@ def tile_locallyconnected2d_kernel(tc, x, weights, bias, grad_out, out):
         x_grp = keep.tile([P, XCOLS, PACK], BF16, name="x_grp", align_bytes=64)
         x_scales = keep.tile([P, XWIDE], U8, name="x_scales", align_bytes=64)
         x_codes = {}
-        for loc in range(2 * SIDE):
+        for loc in (1, 3, 4, 5):
             x_codes[loc] = keep.tile([P, XWIDE], I32, name="x_codes%d" % loc, align_bytes=64)
-        for loc in range(2 * SIDE, LOCS):
-            x_codes[loc] = x_codes[loc - 2 * SIDE]
+        x_codes[0] = x_codes[6] = x_codes[3]
+        x_codes[7] = x_codes[1]
+        x_codes[2] = x_codes[8] = x_codes[5]
         g_raw = {}
         for t in range(O_TILES):
             g_raw[t] = keep.tile([P, PACK, XCOLS], BF16, name="g_raw%d" % t)
@@ -68,9 +69,9 @@ def tile_locallyconnected2d_kernel(tc, x, weights, bias, grad_out, out):
         nc.gpsimd.memset(x_scales[:].bitcast(F32), 0.0)
         nc.gpsimd.memset(x_codes[4][:, 0:PAD].bitcast(F32), 0.0)
         nc.gpsimd.memset(x_codes[4][:, PAD + XCOLS : XWIDE].bitcast(F32), 0.0)
-        for loc in (3, 5, 0, 1):
+        for loc in (3, 5):
             nc.gpsimd.memset(x_codes[loc][:].bitcast(F32), 0.0)
-        nc.vector.memset(x_codes[2][:], 0)
+        nc.vector.memset(x_codes[1][:], 0)
 
         def regroup_x(engine_copy, c0, c1):
             engine_copy(
@@ -149,6 +150,12 @@ def tile_locallyconnected2d_kernel(tc, x, weights, bias, grad_out, out):
                 nc.vector.tensor_copy(out=taps(x_codes[loc], 2, 3, v0, v1), in_=taps(x_codes[4], 2, 3, v0, v1))
             return job
 
+        def top_job(loc):
+            def job():
+                v0, v1 = valid(loc % SIDE)
+                nc.vector.memset(taps(x_codes[loc], 2, 3, v0, v1), 0)
+            return job
+
         def both(first, second):
             def job():
                 first()
@@ -199,9 +206,9 @@ def tile_locallyconnected2d_kernel(tc, x, weights, bias, grad_out, out):
             if n == 2:
                 return [r[0], first_row[1], q[0], q[1]]
             if n == 3:
-                return [mask_job(0), q[0], mask_job(1), q[1]]
+                return [q[0], both(top_job(0), mask_job(1)), both(q[1], top_job(2))]
             if n == 4:
-                return [mask_job(2), r[0], r[1], q[0], q[1]]
+                return [r[0], r[1], q[0], q[1]]
             if n == 5:
                 return [r[0], turn_job(6), r[1], turn_job(7), both(q[0], q[1]), turn_job(8)]
             return r + q

@@ -41,7 +41,7 @@ def tile_locallyconnected2d_kernel(tc, x, weights, bias, grad_out, out):
         psum = stack.enter_context(tc.psum_pool(name="psum", bufs=8))
         stack.enter_context(tc.manual_schedule())
 
-        x_raw = keep.tile([P, PACK, XCOLS], BF16, name="x_raw")
+        x_raw = keep.tile([P, PACK, XCOLS], BF16, name="x_raw", align_bytes=256)
         x_grp = keep.tile([P, XCOLS, PACK], BF16, name="x_grp", align_bytes=64)
         x_scales = keep.tile([P, XWIDE], U8, name="x_scales", align_bytes=64)
         x_codes = {}
@@ -52,7 +52,7 @@ def tile_locallyconnected2d_kernel(tc, x, weights, bias, grad_out, out):
         x_codes[2] = x_codes[8] = x_codes[5]
         g_raw = {}
         for t in range(O_TILES):
-            g_raw[t] = keep.tile([P, PACK, XCOLS], BF16, name="g_raw%d" % t)
+            g_raw[t] = keep.tile([P, PACK, XCOLS], BF16, name="g_raw%d" % t, align_bytes=256)
         g_grp, g_codes, g_scales = {}, {}, {}
         for n in range(UNITS):
             width = GROUP * P if n < O_TILES else GROUP * 2 * P
@@ -226,7 +226,7 @@ def tile_locallyconnected2d_kernel(tc, x, weights, bias, grad_out, out):
                 el = loc - GROUP * a
                 if n < O_TILES:
                     if n % 2 == 0:
-                        res_of[loc] = outs.tile([P, 2, XCOLS], F32, name="res")
+                        res_of[loc] = outs.tile([P, 2, XCOLS], F32, name="res", align_bytes=256)
                     res = res_of[loc]
                     product(loc, n, el * P, res[:, n % 2, :])
                     nc.sync.dma_start(
@@ -236,7 +236,7 @@ def tile_locallyconnected2d_kernel(tc, x, weights, bias, grad_out, out):
                 else:
                     u = (n - O_TILES) % 2
                     if e == 0:
-                        res_of[loc] = outs.tile([P, 2, XCOLS], F32, name="res")
+                        res_of[loc] = outs.tile([P, 2, XCOLS], F32, name="res", align_bytes=256)
                     res = res_of[loc]
                     product(loc, n, (2 * el + e) * P, res[:, e, :])
                     if e == 1:

@@ -66,12 +66,11 @@ def tile_locallyconnected2d_kernel(tc, x, weights, bias, grad_out, out):
             cols = slice(t * XCOLS, (t + 1) * XCOLS)
             nc.sync.dma_start(out=g_raw[t][:], in_=g_rows[:, :, cols])
 
-        nc.gpsimd.memset(x_scales[:].bitcast(F32), 0.0)
-        nc.gpsimd.memset(x_codes[4][:, 0:PAD].bitcast(F32), 0.0)
-        nc.gpsimd.memset(x_codes[4][:, PAD + XCOLS : XWIDE].bitcast(F32), 0.0)
-        for loc in (3, 5):
-            nc.gpsimd.memset(x_codes[loc][:].bitcast(F32), 0.0)
-        nc.vector.memset(x_codes[1][:], 0)
+        nc.vector.memset(x_scales[:].bitcast(I32), 0)
+        nc.vector.memset(x_codes[4][:, 0:PAD], 0)
+        nc.vector.memset(x_codes[4][:, PAD + XCOLS : XWIDE], 0)
+        for loc in (3, 5, 1):
+            nc.vector.memset(x_codes[loc][:], 0)
 
         def regroup_x(engine_copy, c0, c1):
             engine_copy(

from contextlib import ExitStack

import concourse.mybir as mybir

BF16 = mybir.dt.bfloat16
F32 = mybir.dt.float32
I32 = mybir.dt.int32
U8 = mybir.dt.uint8
E4X4 = mybir.dt.float8_e4m3fn_x4
E5X4 = mybir.dt.float8_e5m2_x4

P = 128
PACK = 4
B, IN_C, OUT_C, SIDE = 512, 128, 512, 3
LOCS = SIDE * SIDE
XCOLS = IN_C * LOCS
O_TILES = OUT_C // P
PAD = 64
WIN = 512
STEP = 384
XWIDE = 2 * STEP + WIN
GROUP = 3
UNITS = 8

FLOPS = 2 * 49 * OUT_C * IN_C * B
BYTES = 2 * B * XCOLS + 2 * B * OUT_C * LOCS + 4 * LOCS * OUT_C * XCOLS

V_SHARE = (18, 18, 18, 18, 6, 6, 3, 2)
RES_BUFS = 6


def valid(loc):
    return max(0, loc - 1), min(SIDE, loc + 2)


def tile_locallyconnected2d_kernel(tc, x, weights, bias, grad_out, out):
    nc = tc.nc
    with ExitStack() as stack:
        keep = stack.enter_context(tc.tile_pool(name="keep", bufs=1))
        outs = stack.enter_context(tc.tile_pool(name="outs", bufs=RES_BUFS))
        psum = stack.enter_context(tc.psum_pool(name="psum", bufs=8))
        stack.enter_context(tc.manual_schedule())

        x_raw = keep.tile([P, PACK, XCOLS], BF16, name="x_raw", align_bytes=256)
        x_grp = keep.tile([P, XCOLS, PACK], BF16, name="x_grp", align_bytes=64)
        x_scales = keep.tile([P, XWIDE], U8, name="x_scales", align_bytes=64)
        x_codes = {}
        for loc in (1, 3, 4, 5):
            x_codes[loc] = keep.tile([P, XWIDE], I32, name="x_codes%d" % loc, align_bytes=64)
        x_codes[0] = x_codes[6] = x_codes[3]
        x_codes[7] = x_codes[1]
        x_codes[2] = x_codes[8] = x_codes[5]
        g_raw = {}
        for t in range(O_TILES):
            g_raw[t] = keep.tile([P, PACK, XCOLS], BF16, name="g_raw%d" % t, align_bytes=256)
        g_grp, g_codes, g_scales = {}, {}, {}
        for n in range(UNITS):
            width = GROUP * P if n < O_TILES else GROUP * 2 * P
            g_grp[n] = keep.tile([P, width * PACK], BF16, name="g_grp%d" % n, align_bytes=64)
            g_codes[n] = keep.tile([P, width], I32, name="g_codes%d" % n, align_bytes=64)
            g_scales[n] = keep.tile([P, width], U8, name="g_scales%d" % n, align_bytes=64)

        nc.sync.dma_start(out=x_raw[:], in_=x.rearrange("(p j) c h w -> p j (c h w)", j=PACK))
        g_rows = grad_out.rearrange("(p j) o h w -> p j (o h w)", j=PACK)
        for t in range(O_TILES):
            cols = slice(t * XCOLS, (t + 1) * XCOLS)
            nc.sync.dma_start(out=g_raw[t][:], in_=g_rows[:, :, cols])

        nc.vector.memset(x_scales[:].bitcast(I32), 0)
        nc.vector.memset(x_codes[4][:, 0:PAD], 0)
        nc.vector.memset(x_codes[4][:, PAD + XCOLS : XWIDE], 0)
        for loc in (3, 5, 1):
            nc.vector.memset(x_codes[loc][:], 0)

        def regroup_x(engine_copy, c0, c1):
            engine_copy(
                out=x_grp[:, c0:c1, :].rearrange("p (c i) t -> p c t i", i=4),
                in_=x_raw[:, :, c0:c1].rearrange("p t (c i) -> p c t i", i=4),
            )

        x_flat = x_grp[:].rearrange("p c t -> p (c t)")

        def quantise_x(c0, c1):
            nc.vector.quantize_mx(
                out=x_codes[4][:, PAD + c0 : PAD + c1].bitcast(E4X4),
                scales=x_scales[:, PAD + c0 : PAD + c1],
                in_=x_flat[:, PACK * c0 : PACK * c1],
            )

        def row_of(n):
            return 1 if n < O_TILES else (0 if n < O_TILES + 2 else 2)

        def regroup_jobs(n):
            a = row_of(n)
            if n < O_TILES:
                def middle():
                    nc.vector.tensor_copy(
                        out=g_grp[n][:].rearrange("p (l o j) -> p o j l", l=GROUP, j=PACK),
                        in_=g_raw[n][:].rearrange("p j (o q) -> p o j q", q=LOCS)[:, :, :, GROUP * a : GROUP * (a + 1)],
                    )
                return [middle]
            u = (n - O_TILES) % 2

            def half(s):
                def job():
                    nc.vector.tensor_copy(
                        out=g_grp[n][:].rearrange("p (l e o j) -> p e o j l", l=GROUP, e=2, j=PACK)[
                            :, :, 64 * s : 64 * (s + 1), :, :
                        ],
                        in_=g_raw[2 * u + s][:].rearrange("p j (o e q) -> p e o j q", e=2, q=LOCS)[
                            :, :, :, :, GROUP * a : GROUP * (a + 1)
                        ],
                    )
                return job

            return [half(0), half(1)]

        def quantise_jobs(n):
            cuts = (0, 256, 384) if n < O_TILES else (0, 512, 768)

            def part(c0, c1):
                def job():
                    nc.vector.quantize_mx(
                        out=g_codes[n][:, c0:c1].bitcast(E5X4),
                        scales=g_scales[n][:, c0:c1],
                        in_=g_grp[n][:, PACK * c0 : PACK * c1],
                    )
                return job

            return [part(cuts[0], cuts[1]), part(cuts[1], cuts[2])]

        def mask_job(loc):
            def job():
                y0, y1 = valid(loc // SIDE)
                v0, v1 = valid(loc % SIDE)
                nc.vector.tensor_copy(
                    out=x_codes[loc][:, PAD : PAD + XCOLS].rearrange("p (c y v) -> p c y v", y=SIDE, v=SIDE)[:, :, y0:y1, v0:v1],
                    in_=x_codes[4][:, PAD : PAD + XCOLS].rearrange("p (c y v) -> p c y v", y=SIDE, v=SIDE)[:, :, y0:y1, v0:v1],
                )
            return job

        def taps(tile, y0, y1, v0, v1):
            return tile[:, PAD : PAD + XCOLS].rearrange("p (c y v) -> p c y v", y=SIDE, v=SIDE)[:, :, y0:y1, v0:v1]

        def turn_job(loc):
            def job():
                v0, v1 = valid(loc % SIDE)
                nc.vector.memset(taps(x_codes[loc], 0, 1, v0, v1), 0)
                nc.vector.tensor_copy(out=taps(x_codes[loc], 2, 3, v0, v1), in_=taps(x_codes[4], 2, 3, v0, v1))
            return job

        def top_job(loc):
            def job():
                v0, v1 = valid(loc % SIDE)
                nc.vector.memset(taps(x_codes[loc], 2, 3, v0, v1), 0)
            return job

        def both(first, second):
            def job():
                first()
                second()
            return job

        count = [0]

        def product(loc, n, col0, dst_row):
            shift = SIDE * (loc // SIDE - 1) + (loc % SIDE - 1)
            every = V_SHARE[n]
            for part in range(3):
                acc = psum.tile([P, WIN], F32, name="acc")
                nc.tensor.matmul_mx(
                    out=acc[:],
                    lhsT=g_codes[n][:, col0 : col0 + P].bitcast(E5X4),
                    lhsT_scale=g_scales[n][:, col0 : col0 + P],
                    rhs=x_codes[loc][:, part * STEP : part * STEP + WIN].bitcast(E4X4),
                    rhs_scale=x_scales[:, part * STEP : part * STEP + WIN],
                    start=True,
                    stop=True,
                )
                src = acc[:, PAD + shift : PAD + shift + STEP]
                dst = dst_row[:, part * STEP : (part + 1) * STEP]
                if count[0] % every == every - 1:
                    nc.vector.tensor_copy(out=dst, in_=src)
                else:
                    nc.scalar.copy(out=dst, in_=src)
                count[0] += 1

        regroup_x(nc.vector.tensor_copy, 0, 512)
        regroup_x(nc.scalar.copy, 512, XCOLS)
        quantise_x(0, 512)
        regroup_jobs(0)[0]()
        quantise_jobs(0)[0]()
        quantise_x(512, 1024)
        quantise_x(1024, XCOLS)
        quantise_jobs(0)[1]()

        def plan(n):
            r = regroup_jobs(n + 1) if n + 1 < UNITS else []
            q = quantise_jobs(n + 1) if n + 1 < UNITS else []
            first_row = regroup_jobs(O_TILES)
            if n == 0:
                return [mask_job(3), mask_job(5), r[0], q[0], q[1]]
            if n == 1:
                return [r[0], first_row[0], q[0], q[1]]
            if n == 2:
                return [r[0], first_row[1], q[0], q[1]]
            if n == 3:
                return [q[0], both(top_job(0), mask_job(1)), both(q[1], top_job(2))]
            if n == 4:
                return [r[0], r[1], q[0], q[1]]
            if n == 5:
                return [r[0], turn_job(6), r[1], turn_job(7), both(q[0], q[1]), turn_job(8)]
            return r + q

        res_of = {}
        for n in range(UNITS):
            jobs = plan(n)
            a = row_of(n)
            if n < O_TILES:
                products = [(4, 0), (3, 0), (5, 0)]
            else:
                products = [(GROUP * a + el, e) for el in range(GROUP) for e in range(2)]
            issued = 0
            for k, (loc, e) in enumerate(products):
                el = loc - GROUP * a
                if n < O_TILES:
                    if n % 2 == 0:
                        res_of[loc] = outs.tile([P, 2, XCOLS], F32, name="res", align_bytes=256)
                    res = res_of[loc]
                    product(loc, n, el * P, res[:, n % 2, :])
                    nc.sync.dma_start(
                        out=out[loc // SIDE, loc % SIDE, n * P : (n + 1) * P].rearrange("o c i j -> o (c i j)"),
                        in_=res[:, n % 2, :],
                    )
                else:
                    u = (n - O_TILES) % 2
                    if e == 0:
                        res_of[loc] = outs.tile([P, 2, XCOLS], F32, name="res", align_bytes=256)
                    res = res_of[loc]
                    product(loc, n, (2 * el + e) * P, res[:, e, :])
                    if e == 1:
                        view = out[loc // SIDE, loc % SIDE].rearrange("(u p e) c i j -> u p e (c i j)", u=2, e=2)
                        nc.sync.dma_start(out=view[u], in_=res[:])
                want = ((k + 1) * len(jobs) + len(products) - 1) // len(products)
                while issued < want:
                    jobs[issued]()
                    issued += 1
